import numpy as np
import ml_dtypes


def mxq(x, axis, fmt="e4m3"):
    dtype, down = {"e4m3": (ml_dtypes.float8_e4m3fn, 7), "e5m2": (ml_dtypes.float8_e5m2, 14)}[fmt]
    v = np.moveaxis(np.asarray(x, np.float32).astype(ml_dtypes.bfloat16).astype(np.float64), axis, -1)
    blocks = v.reshape(v.shape[:-1] + (-1, 32))
    amax = np.abs(blocks).max(-1, keepdims=True)
    byte = np.maximum(np.where(amax > 0, np.frexp(amax)[1] - 1 + 127, 0) - down, 1)
    scale = np.exp2(byte - 127.0)
    codes = (blocks / scale).astype(np.float32).astype(dtype).astype(np.float64)
    return np.moveaxis((codes * scale).reshape(v.shape), -1, axis)


WIDE = False


def mx_kscale(k):
    if not WIDE:
        return np.ones(k)
    levels = np.array([10, -10, 5, -5, 0])
    if k % 512:
        return np.exp2(np.random.permutation(np.resize(levels, k // 32))).repeat(32)
    a = np.empty((k // 512, 16))
    for p in range(k // 512):
        a[p, :8] = np.random.permutation(np.resize(levels, 8))
        for g in range(8):
            far = levels[np.abs(levels - a[p, g]) >= 10]
            a[p, g + 8] = far[np.random.randint(len(far))]
    return np.exp2(a.ravel()).repeat(32)


BF16 = ml_dtypes.bfloat16


def bf(x):
    return np.asarray(x, np.float32).astype(BF16)


def f64(x):
    return np.asarray(x).astype(np.float64)


B, S, HID, NH, NOPE, ROPE, VD, KV_RANK, SW, QB = 1, 2048, 1024, 8, 64, 128, 128, 512, 384, 128
QK = NOPE + ROPE


def rotate_half(x):
    h = x.shape[-1] // 2
    return np.concatenate([-x[..., h:], x[..., :h]], axis=-1)


def rope_tables():
    pos = np.arange(S, dtype=np.float64)
    inv = 1.0 / (10000.0 ** (np.arange(0, ROPE, 2, dtype=np.float64) / ROPE))
    ang = pos[:, None] * inv[None, :]
    ang = np.concatenate([ang, ang], axis=-1)
    return bf(np.broadcast_to(np.cos(ang)[None], (B, S, ROPE))), bf(np.broadcast_to(np.sin(ang)[None], (B, S, ROPE)))


def draw0():
    s = mx_kscale(HID)
    cos, sin = rope_tables()
    return {"hidden_states": bf(np.random.standard_normal((B, S, HID)) * s), "cos": cos, "sin": sin,
            "Wq": bf(np.random.standard_normal((HID, NH * QK)) * 2.0 / np.sqrt(HID) / s[:, None]),
            "bq": bf(np.random.standard_normal(NH * QK) * 0.2)}


def core(hidden_states, cos, sin, Wq, bq):
    q = ((mxq(f64(hidden_states), 2, "e4m3") @ mxq(f64(Wq), 0, "e4m3")) + f64(bq)).reshape(B, S, NH, QK).transpose(0, 2, 1, 3)
    q_nope, q_rope = q[..., :NOPE], q[..., NOPE:]
    c, si = f64(cos)[:, None], f64(sin)[:, None]
    q_rope = q_rope * c + rotate_half(q_rope) * si
    return np.concatenate([q_nope, q_rope], axis=-1)


def e4m3fn_bytes(y):
    return np.clip(np.asarray(y, np.float64), -448.0, 448.0).astype(np.float32).astype(ml_dtypes.float8_e4m3fn).view(np.uint8)


def e4m3fn_values(b):
    return np.asarray(b, np.uint8).view(ml_dtypes.float8_e4m3fn).astype(np.float64)


def setup_inputs():
    d = draw0()
    x0 = np.asarray(d['hidden_states']).astype(np.float64)
    s = (np.max(np.abs(x0), axis=(0, 1), keepdims=True) / 448.0).astype(np.float32)
    out = {}
    for k, v in d.items():
        if k == 'hidden_states':
            out['hidden_states_bytes'] = e4m3fn_bytes(x0 / s.astype(np.float64))
            out['hidden_states_scale'] = s
        else:
            out[k] = v
    return out


def reference(hidden_states_bytes, hidden_states_scale, cos, sin, Wq, bq):
    return core(e4m3fn_values(hidden_states_bytes) * hidden_states_scale.astype(np.float64), cos, sin, Wq, bq)

@@ -1,0 +1,315 @@
+from contextlib import ExitStack
+
+import concourse.mybir as mybir
+from concourse.masks import make_identity
+
+F32 = mybir.dt.float32
+BF16 = mybir.dt.bfloat16
+U8 = mybir.dt.uint8
+U32 = mybir.dt.uint32
+FP8 = mybir.dt.float8_e4m3fn
+FP8X4 = mybir.dt.float8_e4m3fn_x4
+ALU = mybir.AluOpType
+ACT = mybir.ActivationFunctionType
+
+S, HID, NH, NOPE, ROPE = 2048, 1024, 8, 64, 128
+QK = NOPE + ROPE
+P = 128
+NG = 4
+NJ = 4
+NB = 12
+FLOPS = 2 * S * HID * NH * QK
+
+
+def tile_gptossmlaattention_pb_kernel(tc, hidden_states_bytes, hidden_states_scale, cos, sin, Wq, bq, out):
+    nc = tc.nc
+    hb = hidden_states_bytes.rearrange("o (g p j) k -> (o g) p j k", p=P, j=NJ)
+    wv = Wq.rearrange("(g p t) n -> g p t n", p=P, t=4)
+    ov = out.rearrange("o h (g p j) e -> (o g) j p h e", p=P, j=NJ)
+    NT = NG * NJ
+
+    with ExitStack() as ctx:
+        const = ctx.enter_context(tc.tile_pool(name="const", bufs=1))
+        xb_pool = ctx.enter_context(tc.tile_pool(name="xb", bufs=NG))
+        xs_pool = ctx.enter_context(tc.tile_pool(name="xs", bufs=4))
+        xp_pool = ctx.enter_context(tc.tile_pool(name="xp", bufs=3))
+        xg_pool = ctx.enter_context(tc.tile_pool(name="xg", bufs=2))
+        xc_pool = ctx.enter_context(tc.tile_pool(name="xc", bufs=2))
+        wraw_pool = ctx.enter_context(tc.tile_pool(name="wraw", bufs=1))
+        wgrp_pool = ctx.enter_context(tc.tile_pool(name="wgrp", bufs=3))
+        qt_pool = ctx.enter_context(tc.tile_pool(name="qt", bufs=2 * NB))
+        pr_pool = ctx.enter_context(tc.tile_pool(name="pr", bufs=2))
+        ot_pool = ctx.enter_context(tc.tile_pool(name="ot", bufs=3))
+        ps_pool = ctx.enter_context(tc.psum_pool(name="ps", bufs=8))
+
+        ident = const.tile([P, P], F32, name="ident")
+        sc_bc = const.tile([P, HID], F32, name="sc_bc")
+        sc4 = const.tile([P, 2, 4], F32, name="sc4")
+        bias_r = const.tile([P, NH], BF16, name="bias_r")
+        bias_n = const.tile([P, 4], BF16, name="bias_n")
+        tab = const.tile([P, NT, 2, 2, 64], BF16, name="tab")
+        w_codes = const.tile([P, 3, 2, 4 * P], U32, name="w_codes", align_bytes=64)
+        w_scales = const.tile([P, 3, 2, 4 * P], U8, name="w_scales", align_bytes=64)
+
+        xbs = []
+        xss = {}
+        xps = {}
+        xts = {}
+        xgs = {}
+        xcs = {}
+        qts = {}
+
+        def load_x(grp, part=None):
+            if part != 1:
+                xb_new = xb_pool.tile([P, NJ, HID], U8, name="xb")
+                xbs.append(xb_new)
+            if part is None:
+                nc.sync.dma_start(out=xbs[grp][:], in_=hb[grp])
+            else:
+                nc.sync.dma_start(out=xbs[grp][:, 2 * part : 2 * part + 2, :], in_=hb[grp][:, 2 * part : 2 * part + 2, :])
+
+        def widen(m):
+            xs = xs_pool.tile([P, HID], BF16, name="xs")
+            nc.vector.tensor_tensor(out=xs[:], in0=xbs[m // NJ][:, m % NJ, :].bitcast(FP8), in1=sc_bc[:], op=ALU.mult)
+            xss[m] = xs
+
+        def xtr(m):
+            words = xss[m][:].bitcast(F32)
+            xt = ps_pool.tile([P, 2, 2, P], F32, name="ps")
+            for g in range(2):
+                for u in range(2):
+                    nc.tensor.transpose(xt[:, g, u, :], words[:, 256 * g + u : 256 * (g + 1) : 2], ident[:])
+            xts[m] = xt
+
+        def xev(m):
+            grp, j = m // NJ, m % NJ
+            if j == 0:
+                new_xg(grp)
+            nc.scalar.copy(out=xgs[grp][:, :, P * j : P * (j + 1), :], in_=xts[m][:].rearrange("p g u n -> p g n u"))
+
+        def new_xg(grp):
+            xg_new = xg_pool.tile([P, 2, NJ * P, 2], F32, name="xg", align_bytes=64)
+            xgs[grp] = xg_new
+
+        def cast_pair(pp):
+            xp = xp_pool.tile([P, 2, HID], BF16, name="xp")
+            a = 2 * (pp % 2)
+            nc.scalar.copy(
+                out=xp[:].rearrange("p a k -> p (a k)"),
+                in_=xbs[pp // 2][:, a : a + 2, :].rearrange("p a k -> p (a k)").bitcast(FP8),
+            )
+            xps[pp] = xp
+
+        def unit2(un):
+            pp, g = un // 2, un % 2
+            grp = pp // 2
+            if un % 4 == 0:
+                new_xg(grp)
+            xt = ps_pool.tile([P, 2, 2, P], F32, name="ps")
+            for jj in range(2):
+                words = xps[pp][:, jj, :].bitcast(F32)
+                for u in range(2):
+                    nc.tensor.transpose(xt[:, u, jj, :], words[:, 256 * g + u : 256 * (g + 1) : 2], ident[:])
+            c0 = 256 * (pp % 2)
+            nc.vector.tensor_tensor(
+                out=xgs[grp][:, g, c0 : c0 + 256, :].bitcast(BF16).rearrange("p n (u e) -> p n u e", u=2),
+                in0=xt[:].rearrange("p u j n -> p u (j n)").bitcast(BF16).rearrange("p u (n e) -> p n u e", e=2),
+                in1=sc4[:, g, :].rearrange("p (u e) -> p u e", u=2).unsqueeze(1).to_broadcast([P, 256, 2, 2]),
+                op=ALU.mult,
+            )
+
+        def quant_x(grp):
+            xc = xc_pool.tile([P, 2, NJ * P], U32, name="xc", align_bytes=64)
+            xsc = xc_pool.tile([P, 2, NJ * P], U8, name="xsc", align_bytes=64)
+            nc.vector.quantize_mx(
+                out=xc[:].rearrange("p g n -> p (g n)").bitcast(FP8X4),
+                scales=xsc[:].rearrange("p g n -> p (g n)"),
+                in_=xgs[grp][:].rearrange("p g n u -> p (g n u)").bitcast(BF16),
+            )
+            xcs[grp] = (xc, xsc)
+
+        def interleave(eng, dst, src):
+            if eng == "v":
+                nc.vector.tensor_copy(out=dst, in_=src)
+            elif eng == "s":
+                nc.scalar.copy(out=dst, in_=src)
+            else:
+                nc.gpsimd.tensor_scalar(out=dst, in0=src, scalar1=1.0, scalar2=0.0, op0=ALU.mult, op1=ALU.add)
+
+        wraw = {}
+        wgs = {}
+
+        def w_copy(eng, g, c):
+            if c not in wgs:
+                wg_new = wgrp_pool.tile([P, 2, 4 * P, 4], BF16, name="wgrp", align_bytes=64)
+                wgs[c] = wg_new
+            wg = wgs[c][:, g, :, :]
+            if c < 2:
+                interleave(
+                    eng,
+                    wg.rearrange("p (h c) t -> p h c t", h=4),
+                    wraw[(g, c)][:].rearrange("p t (h e) -> p h e t", e=QK)[:, :, NOPE:QK, :],
+                )
+            else:
+                for half in range(2):
+                    interleave(
+                        eng,
+                        wg[:, 256 * half : 256 * (half + 1), :].rearrange("p (h c) t -> p h c t", h=4),
+                        wraw[(g, half)][:].rearrange("p t (h e) -> p h e t", e=QK)[:, :, 0:NOPE, :],
+                    )
+
+        def w_quant(c):
+            nc.vector.quantize_mx(
+                out=w_codes[:, c, :, :].rearrange("p g n -> p (g n)").bitcast(FP8X4),
+                scales=w_scales[:, c, :, :].rearrange("p g n -> p (g n)"),
+                in_=wgs[c][:].rearrange("p g c t -> p (g c t)"),
+            )
+
+        def mx_block(grp, b, c0=0, ncols=NJ * P):
+            xc, xsc = xcs[grp]
+            acc = ps_pool.tile([P, NJ * P], F32, name="ps")
+            for g in range(2):
+                nc.tensor.matmul_mx(
+                    out=acc[:, 0:ncols],
+                    lhsT=w_codes[:, b // 4, g, P * (b % 4) : P * (b % 4 + 1)].bitcast(FP8X4),
+                    lhsT_scale=w_scales[:, b // 4, g, P * (b % 4) : P * (b % 4 + 1)],
+                    rhs=xc[:, g, c0 : c0 + ncols].bitcast(FP8X4),
+                    rhs_scale=xsc[:, g, c0 : c0 + ncols],
+                    start=(g == 0),
+                    stop=(g == 1),
+                )
+            if c0 == 0:
+                qt_new = qt_pool.tile([P, NJ * P], F32, name="qt")
+                qts[(grp, b)] = qt_new
+            bias = bias_r[:, b : b + 1] if b < NH else bias_n[:, b - NH : b - NH + 1]
+            nc.scalar.activation(
+                out=qts[(grp, b)][:, c0 : c0 + ncols], in_=acc[:, 0:ncols], func=ACT.Identity, bias=bias, scale=1.0
+            )
+
+        def back(n):
+            grp, j = n // NJ, n % NJ
+            last = n == NT - 1
+            cols = slice(P * j, P * (j + 1))
+            ot = ot_pool.tile([P, NH, QK], F32, name="ot")
+            pr = pr_pool.tile([P, NH, 2, ROPE], F32, name="pr")
+            qrs = []
+            for half in range(2):
+                qr = ps_pool.tile([P, 4, ROPE], F32, name="ps")
+                for hh in range(4):
+                    nc.tensor.transpose(qr[:, hh, :], qts[(grp, 4 * half + hh)][:, cols], ident[:])
+                qrs.append(qr)
+            qn = ps_pool.tile([P, 4, P], F32, name="ps")
+            for i in range(4):
+                nc.tensor.transpose(qn[:, i, :], qts[(grp, NH + i)][:, cols], ident[:])
+            nc.scalar.copy(out=ot[:, :, 0:NOPE], in_=qn[:].rearrange("p i (a e) -> p (i a) e", a=2))
+            for half in range(2):
+                hs = slice(4 * half, 4 * (half + 1))
+                nc.vector.tensor_tensor(
+                    out=pr[:, hs, :, :],
+                    in0=qrs[half][:].unsqueeze(2).to_broadcast([P, 4, 2, ROPE]),
+                    in1=tab[:, n, :, :, :].rearrange("p r x d -> p r (x d)").unsqueeze(1).to_broadcast([P, 4, 2, ROPE]),
+                    op=ALU.mult,
+                )
+                if last:
+                    eng = nc.gpsimd if half == 0 else nc.vector
+                    eng.tensor_tensor(
+                        out=ot[:, hs, NOPE:QK].rearrange("p h (r d) -> p h r d", r=2),
+                        in0=pr[:, hs, :, 0:64],
+                        in1=pr[:, hs, :, 64:128],
+                        op=ALU.add,
+                    )
+                    nc.sync.dma_start(out=ov[grp, j][:, hs, :], in_=ot[:, hs, :])
+            if not last:
+                nc.gpsimd.tensor_tensor(
+                    out=ot[:, :, NOPE:QK].rearrange("p h (r d) -> p h r d", r=2),
+                    in0=pr[:, :, :, 0:64],
+                    in1=pr[:, :, :, 64:128],
+                    op=ALU.add,
+                )
+                nc.sync.dma_start(out=ov[grp, j], in_=ot[:])
+
+        def load_w(g, half):
+            wr = wraw_pool.tile([P, 4, 4 * QK], BF16, name="wraw%d%d" % (g, half))
+            nc.sync.dma_start(out=wr[:], in_=wv[g][:, :, 4 * QK * half : 4 * QK * (half + 1)])
+            wraw[(g, half)] = wr
+
+        nc.scalar.dma_start(out=sc4[:], in_=hidden_states_scale.rearrange("a b (g p t) -> p (a b g) t", p=P, t=4))
+        load_x(0, 0)
+        load_w(0, 0)
+        load_x(0, 1)
+        load_w(1, 0)
+        load_x(1)
+        load_w(0, 1)
+        load_w(1, 1)
+        with nc.allow_non_contiguous_dma(reason="bias, one value to a partition"):
+            nc.sync.dma_start(out=bias_r[:], in_=bq.rearrange("(h e) -> e h", e=QK)[NOPE:QK, :])
+            for a in range(2):
+                nc.sync.dma_start(
+                    out=bias_n[64 * a : 64 * (a + 1), :],
+                    in_=bq.rearrange("(i a e) -> a e i", a=2, e=QK)[a, 0:NOPE, :],
+                )
+        nc.sync.dma_start(out=sc_bc[:], in_=hidden_states_scale.rearrange("a b k -> (a b k)").partition_broadcast(P))
+        load_x(2)
+        cs_raw = wraw_pool.tile([P, NG, NJ * ROPE], BF16, name="cs_raw")
+        sn_raw = wraw_pool.tile([P, NG, NJ * ROPE], BF16, name="sn_raw")
+        nc.sync.dma_start(out=cs_raw[:], in_=cos.rearrange("o (g p j) d -> p (o g) (j d)", p=P, j=NJ))
+        nc.sync.dma_start(out=sn_raw[:], in_=sin.rearrange("o (g p j) d -> p (o g) (j d)", p=P, j=NJ))
+        load_x(3)
+        make_identity(nc, ident[:])
+
+        with tc.manual_schedule():
+            cast_pair(0)
+            cast_pair(1)
+            w_copy("v", 0, 0)
+            w_copy("g", 1, 0)
+            unit2(0)
+            unit2(1)
+            cast_pair(2)
+            w_copy("g", 0, 2)
+            unit2(2)
+            unit2(3)
+            cast_pair(3)
+            w_copy("g", 1, 2)
+            unit2(4)
+            unit2(5)
+            w_copy("s", 0, 1)
+            unit2(6)
+            unit2(7)
+            w_copy("s", 1, 1)
+            w_quant(0)
+            quant_x(0)
+            for c in range(3):
+                if c > 0:
+                    w_quant(c)
+                for b in range(4 * c, 4 * (c + 1)):
+                    mx_block(0, b)
+            quant_x(1)
+            widen(8)
+            xtr(8)
+            xev(8)
+            widen(9)
+            widen(10)
+            csv = cs_raw[:].rearrange("p g (j d) -> p (g j) d", d=ROPE)
+            snv = sn_raw[:].rearrange("p g (j d) -> p (g j) d", d=ROPE)
+            nc.vector.tensor_copy(out=tab[:, :, 0, 0, :], in_=csv[:, :, 0:64])
+            nc.vector.tensor_scalar(out=tab[:, :, 0, 1, :], in0=snv[:, :, 0:64], scalar1=-1.0, scalar2=None, op0=ALU.mult)
+            nc.vector.tensor_copy(out=tab[:, :, 1, 0, :], in_=snv[:, :, 64:128])
+            nc.vector.tensor_copy(out=tab[:, :, 1, 1, :], in_=csv[:, :, 64:128])
+
+            halves = [(b, 256 * hf) for hf in range(2) for b in range(NB)]
+            for n in range(NT):
+                grp, j = n // NJ, n % NJ
+                back(n)
+                if j == 3 and grp + 2 < NG:
+                    quant_x(grp + 2)
+                if n + 11 < NT:
+                    widen(n + 11)
+                if grp + 1 < NG - 1:
+                    for b in range(3 * j, 3 * (j + 1)):
+                        mx_block(grp + 1, b)
+                if 8 <= n < 14:
+                    for b, c0 in halves[4 * (n - 8) : 4 * (n - 7)]:
+                        mx_block(NG - 1, b, c0, 256)
+                if n + 9 < NT:
+                    xtr(n + 9)
+                    xev(n + 9)

@@ -302,8 +302,10 @@ def tile_gptossmlaattention_pb_kernel(tc, hidden_states_bytes, hidden_states_sca
                 back(n)
                 if j == 3 and grp + 2 < NG:
                     quant_x(grp + 2)
-                if n + 11 < NT:
+                if n < 3:
                     widen(n + 11)
+                if n in (4, 5):
+                    widen(n + 10)
                 if grp + 1 < NG - 1:
                     for b in range(3 * j, 3 * (j + 1)):
                         mx_block(grp + 1, b)

@@ -188,7 +188,7 @@ def tile_gptossmlaattention_pb_kernel(tc, hidden_states_bytes, hidden_states_sca
 
         def back(n):
             grp, j = n // NJ, n % NJ
-            last = n == NT - 1
+            last = n >= NT - 2
             cols = slice(P * j, P * (j + 1))
             ot = ot_pool.tile([P, NH, QK], F32, name="ot")
             pr = pr_pool.tile([P, NH, 2, ROPE], F32, name="pr")

@@ -100,7 +100,9 @@ def tile_gptossmlaattention_pb_kernel(tc, hidden_states_bytes, hidden_states_sca
             )
             xps[pp] = xp
 
-        def unit2(un):
+        xt2 = {}
+
+        def unit2(un, split=False):
             pp, g = un // 2, un % 2
             grp = pp // 2
             if un % 4 == 0:
@@ -110,6 +112,14 @@ def tile_gptossmlaattention_pb_kernel(tc, hidden_states_bytes, hidden_states_sca
                 words = xps[pp][:, jj, :].bitcast(F32)
                 for u in range(2):
                     nc.tensor.transpose(xt[:, u, jj, :], words[:, 256 * g + u : 256 * (g + 1) : 2], ident[:])
+            xt2[un] = xt
+            if not split:
+                unit2_out(un)
+
+        def unit2_out(un):
+            pp, g = un // 2, un % 2
+            grp = pp // 2
+            xt = xt2[un]
             c0 = 256 * (pp % 2)
             nc.vector.tensor_tensor(
                 out=xgs[grp][:, g, c0 : c0 + 256, :].bitcast(BF16).rearrange("p n (u e) -> p n u e", u=2),
@@ -165,7 +175,9 @@ def tile_gptossmlaattention_pb_kernel(tc, hidden_states_bytes, hidden_states_sca
                 in_=wgs[c][:].rearrange("p g c t -> p (g c t)"),
             )
 
-        def mx_block(grp, b, c0=0, ncols=NJ * P):
+        accs = {}
+
+        def mx_block(grp, b, c0=0, ncols=NJ * P, late=False):
             xc, xsc = xcs[grp]
             acc = ps_pool.tile([P, NJ * P], F32, name="ps")
             for g in range(2):
@@ -178,6 +190,12 @@ def tile_gptossmlaattention_pb_kernel(tc, hidden_states_bytes, hidden_states_sca
                     start=(g == 0),
                     stop=(g == 1),
                 )
+            if late:
+                accs[b] = acc
+            else:
+                mx_out(grp, b, acc, c0, ncols)
+
+        def mx_out(grp, b, acc, c0=0, ncols=NJ * P):
             if c0 == 0:
                 qt_new = qt_pool.tile([P, NJ * P], F32, name="qt")
                 qts[(grp, b)] = qt_new
@@ -270,19 +288,26 @@ def tile_gptossmlaattention_pb_kernel(tc, hidden_states_bytes, hidden_states_sca
             unit2(3)
             cast_pair(3)
             w_copy("g", 1, 2)
-            unit2(4)
-            unit2(5)
-            w_copy("s", 0, 1)
-            unit2(6)
-            unit2(7)
-            w_copy("s", 1, 1)
+            for un in range(4, 8):
+                unit2(un, split=True)
             w_quant(0)
             quant_x(0)
-            for c in range(3):
-                if c > 0:
-                    w_quant(c)
-                for b in range(4 * c, 4 * (c + 1)):
-                    mx_block(0, b)
+            for b in range(0, 4):
+                mx_block(0, b, late=True)
+            unit2_out(4)
+            unit2_out(5)
+            w_copy("s", 0, 1)
+            unit2_out(6)
+            unit2_out(7)
+            w_copy("s", 1, 1)
+            w_quant(2)
+            for b in range(0, 4):
+                mx_out(0, b, accs[b])
+            for b in range(8, 12):
+                mx_block(0, b)
+            w_quant(1)
+            for b in range(4, 8):
+                mx_block(0, b)
             quant_x(1)
             widen(8)
             xtr(8)

@@ -27,6 +27,8 @@ def tile_gptossmlaattention_pb_kernel(tc, hidden_states_bytes, hidden_states_sca
     wv = Wq.rearrange("(g p t) n -> g p t n", p=P, t=4)
     ov = out.rearrange("o h (g p j) e -> (o g) j p h e", p=P, j=NJ)
     NT = NG * NJ
+    NA = NT - NJ
+    ovh = out.rearrange("o h (g p j) e -> (o g) p h j e", p=P, j=NJ)
 
     with ExitStack() as ctx:
         const = ctx.enter_context(tc.tile_pool(name="const", bufs=1))
@@ -43,6 +45,10 @@ def tile_gptossmlaattention_pb_kernel(tc, hidden_states_bytes, hidden_states_sca
         ps_pool = ctx.enter_context(tc.psum_pool(name="ps", bufs=8))
 
         ident = const.tile([P, P], F32, name="ident")
+        identb = const.tile([P, P], BF16, name="identb")
+        perm = const.tile([P, P], F32, name="perm")
+        snx = const.tile([P, NJ, ROPE], BF16, name="snx")
+        tabt = const.tile([P, 2, NJ * P], BF16, name="tabt")
         sc_bc = const.tile([P, HID], F32, name="sc_bc")
         sc4 = const.tile([P, 2, 4], F32, name="sc4")
         bias_r = const.tile([P, NH], BF16, name="bias_r")
@@ -206,7 +212,7 @@ def tile_gptossmlaattention_pb_kernel(tc, hidden_states_bytes, hidden_states_sca
 
         def back(n):
             grp, j = n // NJ, n % NJ
-            last = n >= NT - 2
+            last = n >= NT
             cols = slice(P * j, P * (j + 1))
             ot = ot_pool.tile([P, NH, QK], F32, name="ot")
             pr = pr_pool.tile([P, NH, 2, ROPE], F32, name="pr")
@@ -245,6 +251,61 @@ def tile_gptossmlaattention_pb_kernel(tc, hidden_states_bytes, hidden_states_sca
                     op=ALU.add,
                 )
                 nc.sync.dma_start(out=ov[grp, j], in_=ot[:])
+
+        def turn_prep():
+            nc.scalar.copy(out=identb[:], in_=ident[:])
+            nc.scalar.copy(out=perm[:, 0:64], in_=ident[:, 64:128])
+            nc.scalar.copy(out=perm[:, 64:128], in_=ident[:, 0:64])
+            nc.scalar.copy(out=snx[:, :, 0:64], in_=tab[:, NA:NT, 1, 0, :])
+            nc.scalar.copy(out=snx[:, :, 64:128], in_=tab[:, NA:NT, 0, 1, :])
+
+        def turn_tables():
+            tt = ps_pool.tile([P, 2, NJ, P], BF16, name="ps")
+            for j in range(NJ):
+                nc.tensor.transpose(tt[:, 0, j, :], cs_raw[:, NG - 1, ROPE * j : ROPE * (j + 1)], identb[:])
+            for j in range(NJ):
+                nc.tensor.transpose(tt[:, 1, j, :], snx[:, j, :], identb[:])
+            nc.scalar.copy(out=tabt[:].rearrange("p x n -> p (x n)"), in_=tt[:].rearrange("p x j n -> p (x j n)"))
+
+        abs_ = {}
+        oths = {}
+
+        def head_mx(h):
+            mx_block(NG - 1, h, late=True)
+
+        def head_prod(h):
+            if h % 2 == 0:
+                ab_new = wgrp_pool.tile([P, 2, 2, NJ * P], F32, name="wgrp", align_bytes=64)
+                abs_[h] = ab_new[:, 0, :, :]
+                abs_[h + 1] = ab_new[:, 1, :, :]
+            nc.vector.scalar_tensor_tensor(
+                out=abs_[h],
+                in0=accs[h][:].unsqueeze(1).to_broadcast([P, 2, NJ * P]),
+                scalar=bias_r[:, h : h + 1],
+                in1=tabt[:],
+                op0=ALU.add,
+                op1=ALU.mult,
+            )
+
+        def head_plain(i):
+            oth = wraw_pool.tile([P, 2, NJ, QK], F32, name="wraw%d%d" % (i // 2, i % 2))
+            oths[i] = oth
+            qn = ps_pool.tile([P, NJ, P], F32, name="ps")
+            for j in range(NJ):
+                nc.tensor.transpose(qn[:, j, :], qts[(NG - 1, NH + i)][:, P * j : P * (j + 1)], ident[:])
+            nc.scalar.copy(
+                out=oth[:, :, :, 0:NOPE], in_=qn[:].rearrange("p j (a e) -> p a j e", a=2)
+            )
+
+        def head_out(h):
+            i, a = h // 2, h % 2
+            po = ps_pool.tile([P, NJ, ROPE], F32, name="ps")
+            for j in range(NJ):
+                cols = slice(P * j, P * (j + 1))
+                nc.tensor.matmul(po[:, j, :], lhsT=abs_[h][:, 0, cols], rhs=ident[:], is_transpose=True, start=True, stop=False)
+                nc.tensor.matmul(po[:, j, :], lhsT=abs_[h][:, 1, cols], rhs=perm[:], is_transpose=True, start=False, stop=True)
+            nc.scalar.copy(out=oths[i][:, a, :, NOPE:QK], in_=po[:])
+            nc.sync.dma_start(out=ovh[NG - 1][:, h, :, :], in_=oths[i][:, a, :, :])
 
         def load_w(g, half):
             wr = wraw_pool.tile([P, 4, 4 * QK], BF16, name="wraw%d%d" % (g, half))
@@ -321,8 +382,7 @@ def tile_gptossmlaattention_pb_kernel(tc, hidden_states_bytes, hidden_states_sca
             nc.vector.tensor_copy(out=tab[:, :, 1, 0, :], in_=snv[:, :, 64:128])
             nc.vector.tensor_copy(out=tab[:, :, 1, 1, :], in_=csv[:, :, 64:128])
 
-            halves = [(b, 256 * hf) for hf in range(2) for b in range(NB)]
-            for n in range(NT):
+            for n in range(NA):
                 grp, j = n // NJ, n % NJ
                 back(n)
                 if j == 3 and grp + 2 < NG:
@@ -334,9 +394,28 @@ def tile_gptossmlaattention_pb_kernel(tc, hidden_states_bytes, hidden_states_sca
                 if grp + 1 < NG - 1:
                     for b in range(3 * j, 3 * (j + 1)):
                         mx_block(grp + 1, b)
-                if 8 <= n < 14:
-                    for b, c0 in halves[4 * (n - 8) : 4 * (n - 7)]:
-                        mx_block(NG - 1, b, c0, 256)
+                if n in (8, 9):
+                    for b in range(2 * n - 8, 2 * n - 6):
+                        mx_block(NG - 1, b)
+                if n == 8:
+                    turn_prep()
+                if n == 9:
+                    turn_tables()
+                if n == 10:
+                    head_plain(0)
+                    head_plain(1)
+                    head_plain(2)
+                    head_plain(3)
+                if n == 11:
+                    head_mx(0)
+                    head_mx(1)
+                    head_mx(2)
                 if n + 9 < NT:
                     xtr(n + 9)
                     xev(n + 9)
+            LEAD = 3
+            for h in range(NH):
+                head_prod(h)
+                if h + LEAD < NH:
+                    head_mx(h + LEAD)
+                head_out(h)

@@ -53,7 +53,7 @@ def tile_gptossmlaattention_pb_kernel(tc, hidden_states_bytes, hidden_states_sca
         sc4 = const.tile([P, 2, 4], F32, name="sc4")
         bias_r = const.tile([P, NH], BF16, name="bias_r")
         bias_n = const.tile([P, 4], BF16, name="bias_n")
-        tab = const.tile([P, NT, 2, 2, 64], BF16, name="tab")
+        tab = const.tile([P, NA, 2, 2, 64], BF16, name="tab")
         w_codes = const.tile([P, 3, 2, 4 * P], U32, name="w_codes", align_bytes=64)
         w_scales = const.tile([P, 3, 2, 4 * P], U8, name="w_scales", align_bytes=64)
 
@@ -106,12 +106,35 @@ def tile_gptossmlaattention_pb_kernel(tc, hidden_states_bytes, hidden_states_sca
             )
             xps[pp] = xp
 
+        def cast_tile(m):
+            if m % 2 == 0:
+                xp_new = xp_pool.tile([P, 2, HID], BF16, name="xp")
+                xps[m // 2] = xp_new
+            nc.scalar.copy(out=xps[m // 2][:, m % 2, :], in_=xbs[m // NJ][:, m % NJ, :].bitcast(FP8))
+
+        def tile1(m):
+            grp, j = m // NJ, m % NJ
+            if j == 0:
+                new_xg(grp)
+            words = xps[m // 2][:, m % 2, :].bitcast(F32)
+            xt = ps_pool.tile([P, 2, 2, P], F32, name="ps")
+            for g in range(2):
+                for u in range(2):
+                    nc.tensor.transpose(xt[:, g, u, :], words[:, 256 * g + u : 256 * (g + 1) : 2], ident[:])
+            for g in range(2):
+                nc.vector.tensor_tensor(
+                    out=xgs[grp][:, g, P * j : P * (j + 1), :].bitcast(BF16).rearrange("p n (u e) -> p n u e", u=2),
+                    in0=xt[:, g, :, :].bitcast(BF16).rearrange("p u (n e) -> p n u e", e=2),
+                    in1=sc4[:, g, :].rearrange("p (u e) -> p u e", u=2).unsqueeze(1).to_broadcast([P, P, 2, 2]),
+                    op=ALU.mult,
+                )
+
         xt2 = {}
 
         def unit2(un, split=False):
             pp, g = un // 2, un % 2
             grp = pp // 2
-            if un % 4 == 0:
+            if un % 4 == 0 and grp > 0:
                 new_xg(grp)
             xt = ps_pool.tile([P, 2, 2, P], F32, name="ps")
             for jj in range(2):
@@ -212,7 +235,7 @@ def tile_gptossmlaattention_pb_kernel(tc, hidden_states_bytes, hidden_states_sca
 
         def back(n):
             grp, j = n // NJ, n % NJ
-            last = n >= NT
+            last = n >= NA - 2
             cols = slice(P * j, P * (j + 1))
             ot = ot_pool.tile([P, NH, QK], F32, name="ot")
             pr = pr_pool.tile([P, NH, 2, ROPE], F32, name="pr")
@@ -235,8 +258,7 @@ def tile_gptossmlaattention_pb_kernel(tc, hidden_states_bytes, hidden_states_sca
                     op=ALU.mult,
                 )
                 if last:
-                    eng = nc.gpsimd if half == 0 else nc.vector
-                    eng.tensor_tensor(
+                    nc.gpsimd.tensor_tensor(
                         out=ot[:, hs, NOPE:QK].rearrange("p h (r d) -> p h r d", r=2),
                         in0=pr[:, hs, :, 0:64],
                         in1=pr[:, hs, :, 64:128],
@@ -256,8 +278,9 @@ def tile_gptossmlaattention_pb_kernel(tc, hidden_states_bytes, hidden_states_sca
             nc.scalar.copy(out=identb[:], in_=ident[:])
             nc.scalar.copy(out=perm[:, 0:64], in_=ident[:, 64:128])
             nc.scalar.copy(out=perm[:, 64:128], in_=ident[:, 0:64])
-            nc.scalar.copy(out=snx[:, :, 0:64], in_=tab[:, NA:NT, 1, 0, :])
-            nc.scalar.copy(out=snx[:, :, 64:128], in_=tab[:, NA:NT, 0, 1, :])
+            sn3 = sn_raw[:, NG - 1, :].rearrange("p (j d) -> p j d", d=ROPE)
+            nc.scalar.copy(out=snx[:, :, 0:64], in_=sn3[:, :, 64:128])
+            nc.scalar.activation(out=snx[:, :, 64:128], in_=sn3[:, :, 0:64], func=ACT.Copy, scale=-1.0)
 
         def turn_tables():
             tt = ps_pool.tile([P, 2, NJ, P], BF16, name="ps")
@@ -273,16 +296,17 @@ def tile_gptossmlaattention_pb_kernel(tc, hidden_states_bytes, hidden_states_sca
         def head_mx(h):
             mx_block(NG - 1, h, late=True)
 
-        def head_prod(h):
-            if h % 2 == 0:
+        def head_prod(h, t0=0, tn=NJ):
+            if h % 2 == 0 and t0 == 0:
                 ab_new = wgrp_pool.tile([P, 2, 2, NJ * P], F32, name="wgrp", align_bytes=64)
                 abs_[h] = ab_new[:, 0, :, :]
                 abs_[h + 1] = ab_new[:, 1, :, :]
+            toks = slice(P * t0, P * (t0 + tn))
             nc.vector.scalar_tensor_tensor(
-                out=abs_[h],
-                in0=accs[h][:].unsqueeze(1).to_broadcast([P, 2, NJ * P]),
+                out=abs_[h][:, :, toks],
+                in0=accs[h][:, toks].unsqueeze(1).to_broadcast([P, 2, P * tn]),
                 scalar=bias_r[:, h : h + 1],
-                in1=tabt[:],
+                in1=tabt[:, :, toks],
                 op0=ALU.add,
                 op1=ALU.mult,
             )
@@ -297,15 +321,19 @@ def tile_gptossmlaattention_pb_kernel(tc, hidden_states_bytes, hidden_states_sca
                 out=oth[:, :, :, 0:NOPE], in_=qn[:].rearrange("p j (a e) -> p a j e", a=2)
             )
 
-        def head_out(h):
+        def head_out(h, t0=0, tn=NJ, eng=None):
             i, a = h // 2, h % 2
-            po = ps_pool.tile([P, NJ, ROPE], F32, name="ps")
-            for j in range(NJ):
-                cols = slice(P * j, P * (j + 1))
+            po = ps_pool.tile([P, tn, ROPE], F32, name="ps")
+            for j in range(tn):
+                cols = slice(P * (t0 + j), P * (t0 + j + 1))
                 nc.tensor.matmul(po[:, j, :], lhsT=abs_[h][:, 0, cols], rhs=ident[:], is_transpose=True, start=True, stop=False)
                 nc.tensor.matmul(po[:, j, :], lhsT=abs_[h][:, 1, cols], rhs=perm[:], is_transpose=True, start=False, stop=True)
-            nc.scalar.copy(out=oths[i][:, a, :, NOPE:QK], in_=po[:])
-            nc.sync.dma_start(out=ovh[NG - 1][:, h, :, :], in_=oths[i][:, a, :, :])
+            dst = oths[i][:, a, t0 : t0 + tn, NOPE:QK]
+            if eng == "v":
+                nc.vector.tensor_copy(out=dst, in_=po[:])
+            else:
+                nc.scalar.copy(out=dst, in_=po[:])
+            nc.sync.dma_start(out=ovh[NG - 1][:, h, t0 : t0 + tn, :], in_=oths[i][:, a, t0 : t0 + tn, :])
 
         def load_w(g, half):
             wr = wraw_pool.tile([P, 4, 4 * QK], BF16, name="wraw%d%d" % (g, half))
@@ -337,12 +365,13 @@ def tile_gptossmlaattention_pb_kernel(tc, hidden_states_bytes, hidden_states_sca
         make_identity(nc, ident[:])
 
         with tc.manual_schedule():
-            cast_pair(0)
+            cast_tile(0)
+            cast_tile(1)
             cast_pair(1)
+            tile1(0)
+            tile1(1)
             w_copy("v", 0, 0)
-            w_copy("g", 1, 0)
-            unit2(0)
-            unit2(1)
+            w_copy("s", 1, 0)
             cast_pair(2)
             w_copy("g", 0, 2)
             unit2(2)
@@ -377,10 +406,10 @@ def tile_gptossmlaattention_pb_kernel(tc, hidden_states_bytes, hidden_states_sca
             widen(10)
             csv = cs_raw[:].rearrange("p g (j d) -> p (g j) d", d=ROPE)
             snv = sn_raw[:].rearrange("p g (j d) -> p (g j) d", d=ROPE)
-            nc.vector.tensor_copy(out=tab[:, :, 0, 0, :], in_=csv[:, :, 0:64])
-            nc.vector.tensor_scalar(out=tab[:, :, 0, 1, :], in0=snv[:, :, 0:64], scalar1=-1.0, scalar2=None, op0=ALU.mult)
-            nc.vector.tensor_copy(out=tab[:, :, 1, 0, :], in_=snv[:, :, 64:128])
-            nc.vector.tensor_copy(out=tab[:, :, 1, 1, :], in_=csv[:, :, 64:128])
+            nc.vector.tensor_copy(out=tab[:, :, 0, 0, :], in_=csv[:, 0:NA, 0:64])
+            nc.vector.tensor_scalar(out=tab[:, :, 0, 1, :], in0=snv[:, 0:NA, 0:64], scalar1=-1.0, scalar2=None, op0=ALU.mult)
+            nc.vector.tensor_copy(out=tab[:, :, 1, 0, :], in_=snv[:, 0:NA, 64:128])
+            nc.vector.tensor_copy(out=tab[:, :, 1, 1, :], in_=csv[:, 0:NA, 64:128])
 
             for n in range(NA):
                 grp, j = n // NJ, n % NJ
@@ -415,7 +444,10 @@ def tile_gptossmlaattention_pb_kernel(tc, hidden_states_bytes, hidden_states_sca
                     xev(n + 9)
             LEAD = 3
             for h in range(NH):
-                head_prod(h)
+                parts = [(0, 2), (2, 2)] if h == NH - 1 else [(0, NJ)]
+                for i, (t0, tn) in enumerate(parts):
+                    head_prod(h, t0, tn)
                 if h + LEAD < NH:
                     head_mx(h + LEAD)
-                head_out(h)
+                for i, (t0, tn) in enumerate(parts):
+                    head_out(h, t0, tn, "v" if i == 1 else "s")

from contextlib import ExitStack

import concourse.mybir as mybir
from concourse.masks import make_identity

F32 = mybir.dt.float32
BF16 = mybir.dt.bfloat16
U8 = mybir.dt.uint8
U32 = mybir.dt.uint32
FP8 = mybir.dt.float8_e4m3fn
FP8X4 = mybir.dt.float8_e4m3fn_x4
ALU = mybir.AluOpType
ACT = mybir.ActivationFunctionType

S, HID, NH, NOPE, ROPE = 2048, 1024, 8, 64, 128
QK = NOPE + ROPE
P = 128
NG = 4
NJ = 4
NB = 12
FLOPS = 2 * S * HID * NH * QK


def tile_gptossmlaattention_pb_kernel(tc, hidden_states_bytes, hidden_states_scale, cos, sin, Wq, bq, out):
    nc = tc.nc
    hb = hidden_states_bytes.rearrange("o (g p j) k -> (o g) p j k", p=P, j=NJ)
    wv = Wq.rearrange("(g p t) n -> g p t n", p=P, t=4)
    ov = out.rearrange("o h (g p j) e -> (o g) j p h e", p=P, j=NJ)
    NT = NG * NJ
    NA = NT - NJ
    ovh = out.rearrange("o h (g p j) e -> (o g) p h j e", p=P, j=NJ)

    with ExitStack() as ctx:
        const = ctx.enter_context(tc.tile_pool(name="const", bufs=1))
        xb_pool = ctx.enter_context(tc.tile_pool(name="xb", bufs=NG))
        xs_pool = ctx.enter_context(tc.tile_pool(name="xs", bufs=4))
        xp_pool = ctx.enter_context(tc.tile_pool(name="xp", bufs=3))
        xg_pool = ctx.enter_context(tc.tile_pool(name="xg", bufs=2))
        xc_pool = ctx.enter_context(tc.tile_pool(name="xc", bufs=2))
        wraw_pool = ctx.enter_context(tc.tile_pool(name="wraw", bufs=1))
        wgrp_pool = ctx.enter_context(tc.tile_pool(name="wgrp", bufs=3))
        qt_pool = ctx.enter_context(tc.tile_pool(name="qt", bufs=2 * NB))
        pr_pool = ctx.enter_context(tc.tile_pool(name="pr", bufs=2))
        ot_pool = ctx.enter_context(tc.tile_pool(name="ot", bufs=3))
        ps_pool = ctx.enter_context(tc.psum_pool(name="ps", bufs=8))

        ident = const.tile([P, P], F32, name="ident")
        identb = const.tile([P, P], BF16, name="identb")
        perm = const.tile([P, P], F32, name="perm")
        snx = const.tile([P, NJ, ROPE], BF16, name="snx")
        tabt = const.tile([P, 2, NJ * P], BF16, name="tabt")
        sc_bc = const.tile([P, HID], F32, name="sc_bc")
        sc4 = const.tile([P, 2, 4], F32, name="sc4")
        bias_r = const.tile([P, NH], BF16, name="bias_r")
        bias_n = const.tile([P, 4], BF16, name="bias_n")
        tab = const.tile([P, NA, 2, 2, 64], BF16, name="tab")
        w_codes = const.tile([P, 3, 2, 4 * P], U32, name="w_codes", align_bytes=64)
        w_scales = const.tile([P, 3, 2, 4 * P], U8, name="w_scales", align_bytes=64)

        xbs = []
        xss = {}
        xps = {}
        xts = {}
        xgs = {}
        xcs = {}
        qts = {}

        def load_x(grp, part=None):
            if part != 1:
                xb_new = xb_pool.tile([P, NJ, HID], U8, name="xb")
                xbs.append(xb_new)
            if part is None:
                nc.sync.dma_start(out=xbs[grp][:], in_=hb[grp])
            else:
                nc.sync.dma_start(out=xbs[grp][:, 2 * part : 2 * part + 2, :], in_=hb[grp][:, 2 * part : 2 * part + 2, :])

        def widen(m):
            xs = xs_pool.tile([P, HID], BF16, name="xs")
            nc.vector.tensor_tensor(out=xs[:], in0=xbs[m // NJ][:, m % NJ, :].bitcast(FP8), in1=sc_bc[:], op=ALU.mult)
            xss[m] = xs

        def xtr(m):
            words = xss[m][:].bitcast(F32)
            xt = ps_pool.tile([P, 2, 2, P], F32, name="ps")
            for g in range(2):
                for u in range(2):
                    nc.tensor.transpose(xt[:, g, u, :], words[:, 256 * g + u : 256 * (g + 1) : 2], ident[:])
            xts[m] = xt

        def xev(m):
            grp, j = m // NJ, m % NJ
            if j == 0:
                new_xg(grp)
            nc.scalar.copy(out=xgs[grp][:, :, P * j : P * (j + 1), :], in_=xts[m][:].rearrange("p g u n -> p g n u"))

        def new_xg(grp):
            xg_new = xg_pool.tile([P, 2, NJ * P, 2], F32, name="xg", align_bytes=64)
            xgs[grp] = xg_new

        def cast_pair(pp):
            xp = xp_pool.tile([P, 2, HID], BF16, name="xp")
            a = 2 * (pp % 2)
            nc.scalar.copy(
                out=xp[:].rearrange("p a k -> p (a k)"),
                in_=xbs[pp // 2][:, a : a + 2, :].rearrange("p a k -> p (a k)").bitcast(FP8),
            )
            xps[pp] = xp

        def cast_tile(m):
            if m % 2 == 0:
                xp_new = xp_pool.tile([P, 2, HID], BF16, name="xp")
                xps[m // 2] = xp_new
            nc.scalar.copy(out=xps[m // 2][:, m % 2, :], in_=xbs[m // NJ][:, m % NJ, :].bitcast(FP8))

        def tile1(m):
            grp, j = m // NJ, m % NJ
            if j == 0:
                new_xg(grp)
            words = xps[m // 2][:, m % 2, :].bitcast(F32)
            xt = ps_pool.tile([P, 2, 2, P], F32, name="ps")
            for g in range(2):
                for u in range(2):
                    nc.tensor.transpose(xt[:, g, u, :], words[:, 256 * g + u : 256 * (g + 1) : 2], ident[:])
            for g in range(2):
                nc.vector.tensor_tensor(
                    out=xgs[grp][:, g, P * j : P * (j + 1), :].bitcast(BF16).rearrange("p n (u e) -> p n u e", u=2),
                    in0=xt[:, g, :, :].bitcast(BF16).rearrange("p u (n e) -> p n u e", e=2),
                    in1=sc4[:, g, :].rearrange("p (u e) -> p u e", u=2).unsqueeze(1).to_broadcast([P, P, 2, 2]),
                    op=ALU.mult,
                )

        xt2 = {}

        def unit2(un, split=False):
            pp, g = un // 2, un % 2
            grp = pp // 2
            if un % 4 == 0 and grp > 0:
                new_xg(grp)
            xt = ps_pool.tile([P, 2, 2, P], F32, name="ps")
            for jj in range(2):
                words = xps[pp][:, jj, :].bitcast(F32)
                for u in range(2):
                    nc.tensor.transpose(xt[:, u, jj, :], words[:, 256 * g + u : 256 * (g + 1) : 2], ident[:])
            xt2[un] = xt
            if not split:
                unit2_out(un)

        def unit2_out(un):
            pp, g = un // 2, un % 2
            grp = pp // 2
            xt = xt2[un]
            c0 = 256 * (pp % 2)
            nc.vector.tensor_tensor(
                out=xgs[grp][:, g, c0 : c0 + 256, :].bitcast(BF16).rearrange("p n (u e) -> p n u e", u=2),
                in0=xt[:].rearrange("p u j n -> p u (j n)").bitcast(BF16).rearrange("p u (n e) -> p n u e", e=2),
                in1=sc4[:, g, :].rearrange("p (u e) -> p u e", u=2).unsqueeze(1).to_broadcast([P, 256, 2, 2]),
                op=ALU.mult,
            )

        def quant_x(grp):
            xc = xc_pool.tile([P, 2, NJ * P], U32, name="xc", align_bytes=64)
            xsc = xc_pool.tile([P, 2, NJ * P], U8, name="xsc", align_bytes=64)
            nc.vector.quantize_mx(
                out=xc[:].rearrange("p g n -> p (g n)").bitcast(FP8X4),
                scales=xsc[:].rearrange("p g n -> p (g n)"),
                in_=xgs[grp][:].rearrange("p g n u -> p (g n u)").bitcast(BF16),
            )
            xcs[grp] = (xc, xsc)

        def interleave(eng, dst, src):
            if eng == "v":
                nc.vector.tensor_copy(out=dst, in_=src)
            elif eng == "s":
                nc.scalar.copy(out=dst, in_=src)
            else:
                nc.gpsimd.tensor_scalar(out=dst, in0=src, scalar1=1.0, scalar2=0.0, op0=ALU.mult, op1=ALU.add)

        wraw = {}
        wgs = {}

        def w_copy(eng, g, c):
            if c not in wgs:
                wg_new = wgrp_pool.tile([P, 2, 4 * P, 4], BF16, name="wgrp", align_bytes=64)
                wgs[c] = wg_new
            wg = wgs[c][:, g, :, :]
            if c < 2:
                interleave(
                    eng,
                    wg.rearrange("p (h c) t -> p h c t", h=4),
                    wraw[(g, c)][:].rearrange("p t (h e) -> p h e t", e=QK)[:, :, NOPE:QK, :],
                )
            else:
                for half in range(2):
                    interleave(
                        eng,
                        wg[:, 256 * half : 256 * (half + 1), :].rearrange("p (h c) t -> p h c t", h=4),
                        wraw[(g, half)][:].rearrange("p t (h e) -> p h e t", e=QK)[:, :, 0:NOPE, :],
                    )

        def w_quant(c):
            nc.vector.quantize_mx(
                out=w_codes[:, c, :, :].rearrange("p g n -> p (g n)").bitcast(FP8X4),
                scales=w_scales[:, c, :, :].rearrange("p g n -> p (g n)"),
                in_=wgs[c][:].rearrange("p g c t -> p (g c t)"),
            )

        accs = {}

        def mx_block(grp, b, c0=0, ncols=NJ * P, late=False):
            xc, xsc = xcs[grp]
            acc = ps_pool.tile([P, NJ * P], F32, name="ps")
            for g in range(2):
                nc.tensor.matmul_mx(
                    out=acc[:, 0:ncols],
                    lhsT=w_codes[:, b // 4, g, P * (b % 4) : P * (b % 4 + 1)].bitcast(FP8X4),
                    lhsT_scale=w_scales[:, b // 4, g, P * (b % 4) : P * (b % 4 + 1)],
                    rhs=xc[:, g, c0 : c0 + ncols].bitcast(FP8X4),
                    rhs_scale=xsc[:, g, c0 : c0 + ncols],
                    start=(g == 0),
                    stop=(g == 1),
                )
            if late:
                accs[b] = acc
            else:
                mx_out(grp, b, acc, c0, ncols)

        def mx_out(grp, b, acc, c0=0, ncols=NJ * P):
            if c0 == 0:
                qt_new = qt_pool.tile([P, NJ * P], F32, name="qt")
                qts[(grp, b)] = qt_new
            bias = bias_r[:, b : b + 1] if b < NH else bias_n[:, b - NH : b - NH + 1]
            nc.scalar.activation(
                out=qts[(grp, b)][:, c0 : c0 + ncols], in_=acc[:, 0:ncols], func=ACT.Identity, bias=bias, scale=1.0
            )

        def back(n):
            grp, j = n // NJ, n % NJ
            last = n >= NA - 2
            cols = slice(P * j, P * (j + 1))
            ot = ot_pool.tile([P, NH, QK], F32, name="ot")
            pr = pr_pool.tile([P, NH, 2, ROPE], F32, name="pr")
            qrs = []
            for half in range(2):
                qr = ps_pool.tile([P, 4, ROPE], F32, name="ps")
                for hh in range(4):
                    nc.tensor.transpose(qr[:, hh, :], qts[(grp, 4 * half + hh)][:, cols], ident[:])
                qrs.append(qr)
            qn = ps_pool.tile([P, 4, P], F32, name="ps")
            for i in range(4):
                nc.tensor.transpose(qn[:, i, :], qts[(grp, NH + i)][:, cols], ident[:])
            nc.scalar.copy(out=ot[:, :, 0:NOPE], in_=qn[:].rearrange("p i (a e) -> p (i a) e", a=2))
            for half in range(2):
                hs = slice(4 * half, 4 * (half + 1))
                nc.vector.tensor_tensor(
                    out=pr[:, hs, :, :],
                    in0=qrs[half][:].unsqueeze(2).to_broadcast([P, 4, 2, ROPE]),
                    in1=tab[:, n, :, :, :].rearrange("p r x d -> p r (x d)").unsqueeze(1).to_broadcast([P, 4, 2, ROPE]),
                    op=ALU.mult,
                )
                if last:
                    nc.gpsimd.tensor_tensor(
                        out=ot[:, hs, NOPE:QK].rearrange("p h (r d) -> p h r d", r=2),
                        in0=pr[:, hs, :, 0:64],
                        in1=pr[:, hs, :, 64:128],
                        op=ALU.add,
                    )
                    nc.sync.dma_start(out=ov[grp, j][:, hs, :], in_=ot[:, hs, :])
            if not last:
                nc.gpsimd.tensor_tensor(
                    out=ot[:, :, NOPE:QK].rearrange("p h (r d) -> p h r d", r=2),
                    in0=pr[:, :, :, 0:64],
                    in1=pr[:, :, :, 64:128],
                    op=ALU.add,
                )
                nc.sync.dma_start(out=ov[grp, j], in_=ot[:])

        def turn_prep():
            nc.scalar.copy(out=identb[:], in_=ident[:])
            nc.scalar.copy(out=perm[:, 0:64], in_=ident[:, 64:128])
            nc.scalar.copy(out=perm[:, 64:128], in_=ident[:, 0:64])
            sn3 = sn_raw[:, NG - 1, :].rearrange("p (j d) -> p j d", d=ROPE)
            nc.scalar.copy(out=snx[:, :, 0:64], in_=sn3[:, :, 64:128])
            nc.scalar.activation(out=snx[:, :, 64:128], in_=sn3[:, :, 0:64], func=ACT.Copy, scale=-1.0)

        def turn_tables():
            tt = ps_pool.tile([P, 2, NJ, P], BF16, name="ps")
            for j in range(NJ):
                nc.tensor.transpose(tt[:, 0, j, :], cs_raw[:, NG - 1, ROPE * j : ROPE * (j + 1)], identb[:])
            for j in range(NJ):
                nc.tensor.transpose(tt[:, 1, j, :], snx[:, j, :], identb[:])
            nc.scalar.copy(out=tabt[:].rearrange("p x n -> p (x n)"), in_=tt[:].rearrange("p x j n -> p (x j n)"))

        abs_ = {}
        oths = {}

        def head_mx(h):
            mx_block(NG - 1, h, late=True)

        def head_prod(h, t0=0, tn=NJ):
            if h % 2 == 0 and t0 == 0:
                ab_new = wgrp_pool.tile([P, 2, 2, NJ * P], F32, name="wgrp", align_bytes=64)
                abs_[h] = ab_new[:, 0, :, :]
                abs_[h + 1] = ab_new[:, 1, :, :]
            toks = slice(P * t0, P * (t0 + tn))
            nc.vector.scalar_tensor_tensor(
                out=abs_[h][:, :, toks],
                in0=accs[h][:, toks].unsqueeze(1).to_broadcast([P, 2, P * tn]),
                scalar=bias_r[:, h : h + 1],
                in1=tabt[:, :, toks],
                op0=ALU.add,
                op1=ALU.mult,
            )

        def head_plain(i):
            oth = wraw_pool.tile([P, 2, NJ, QK], F32, name="wraw%d%d" % (i // 2, i % 2))
            oths[i] = oth
            qn = ps_pool.tile([P, NJ, P], F32, name="ps")
            for j in range(NJ):
                nc.tensor.transpose(qn[:, j, :], qts[(NG - 1, NH + i)][:, P * j : P * (j + 1)], ident[:])
            nc.scalar.copy(
                out=oth[:, :, :, 0:NOPE], in_=qn[:].rearrange("p j (a e) -> p a j e", a=2)
            )

        def head_out(h, t0=0, tn=NJ, eng=None):
            i, a = h // 2, h % 2
            po = ps_pool.tile([P, tn, ROPE], F32, name="ps")
            for j in range(tn):
                cols = slice(P * (t0 + j), P * (t0 + j + 1))
                nc.tensor.matmul(po[:, j, :], lhsT=abs_[h][:, 0, cols], rhs=ident[:], is_transpose=True, start=True, stop=False)
                nc.tensor.matmul(po[:, j, :], lhsT=abs_[h][:, 1, cols], rhs=perm[:], is_transpose=True, start=False, stop=True)
            dst = oths[i][:, a, t0 : t0 + tn, NOPE:QK]
            if eng == "v":
                nc.vector.tensor_copy(out=dst, in_=po[:])
            else:
                nc.scalar.copy(out=dst, in_=po[:])
            nc.sync.dma_start(out=ovh[NG - 1][:, h, t0 : t0 + tn, :], in_=oths[i][:, a, t0 : t0 + tn, :])

        def load_w(g, half):
            wr = wraw_pool.tile([P, 4, 4 * QK], BF16, name="wraw%d%d" % (g, half))
            nc.sync.dma_start(out=wr[:], in_=wv[g][:, :, 4 * QK * half : 4 * QK * (half + 1)])
            wraw[(g, half)] = wr

        nc.scalar.dma_start(out=sc4[:], in_=hidden_states_scale.rearrange("a b (g p t) -> p (a b g) t", p=P, t=4))
        load_x(0, 0)
        load_w(0, 0)
        load_x(0, 1)
        load_w(1, 0)
        load_x(1)
        load_w(0, 1)
        load_w(1, 1)
        with nc.allow_non_contiguous_dma(reason="bias, one value to a partition"):
            nc.sync.dma_start(out=bias_r[:], in_=bq.rearrange("(h e) -> e h", e=QK)[NOPE:QK, :])
            for a in range(2):
                nc.sync.dma_start(
                    out=bias_n[64 * a : 64 * (a + 1), :],
                    in_=bq.rearrange("(i a e) -> a e i", a=2, e=QK)[a, 0:NOPE, :],
                )
        nc.sync.dma_start(out=sc_bc[:], in_=hidden_states_scale.rearrange("a b k -> (a b k)").partition_broadcast(P))
        load_x(2)
        cs_raw = wraw_pool.tile([P, NG, NJ * ROPE], BF16, name="cs_raw")
        sn_raw = wraw_pool.tile([P, NG, NJ * ROPE], BF16, name="sn_raw")
        nc.sync.dma_start(out=cs_raw[:], in_=cos.rearrange("o (g p j) d -> p (o g) (j d)", p=P, j=NJ))
        nc.sync.dma_start(out=sn_raw[:], in_=sin.rearrange("o (g p j) d -> p (o g) (j d)", p=P, j=NJ))
        load_x(3)
        make_identity(nc, ident[:])

        with tc.manual_schedule():
            cast_tile(0)
            cast_tile(1)
            cast_pair(1)
            tile1(0)
            tile1(1)
            w_copy("v", 0, 0)
            w_copy("s", 1, 0)
            cast_pair(2)
            w_copy("g", 0, 2)
            unit2(2)
            unit2(3)
            cast_pair(3)
            w_copy("g", 1, 2)
            for un in range(4, 8):
                unit2(un, split=True)
            w_quant(0)
            quant_x(0)
            for b in range(0, 4):
                mx_block(0, b, late=True)
            unit2_out(4)
            unit2_out(5)
            w_copy("s", 0, 1)
            unit2_out(6)
            unit2_out(7)
            w_copy("s", 1, 1)
            w_quant(2)
            for b in range(0, 4):
                mx_out(0, b, accs[b])
            for b in range(8, 12):
                mx_block(0, b)
            w_quant(1)
            for b in range(4, 8):
                mx_block(0, b)
            quant_x(1)
            widen(8)
            xtr(8)
            xev(8)
            widen(9)
            widen(10)
            csv = cs_raw[:].rearrange("p g (j d) -> p (g j) d", d=ROPE)
            snv = sn_raw[:].rearrange("p g (j d) -> p (g j) d", d=ROPE)
            nc.vector.tensor_copy(out=tab[:, :, 0, 0, :], in_=csv[:, 0:NA, 0:64])
            nc.vector.tensor_scalar(out=tab[:, :, 0, 1, :], in0=snv[:, 0:NA, 0:64], scalar1=-1.0, scalar2=None, op0=ALU.mult)
            nc.vector.tensor_copy(out=tab[:, :, 1, 0, :], in_=snv[:, 0:NA, 64:128])
            nc.vector.tensor_copy(out=tab[:, :, 1, 1, :], in_=csv[:, 0:NA, 64:128])

            for n in range(NA):
                grp, j = n // NJ, n % NJ
                back(n)
                if j == 3 and grp + 2 < NG:
                    quant_x(grp + 2)
                if n < 3:
                    widen(n + 11)
                if n in (4, 5):
                    widen(n + 10)
                if grp + 1 < NG - 1:
                    for b in range(3 * j, 3 * (j + 1)):
                        mx_block(grp + 1, b)
                if n in (8, 9):
                    for b in range(2 * n - 8, 2 * n - 6):
                        mx_block(NG - 1, b)
                if n == 8:
                    turn_prep()
                if n == 9:
                    turn_tables()
                if n == 10:
                    head_plain(0)
                    head_plain(1)
                    head_plain(2)
                    head_plain(3)
                if n == 11:
                    head_mx(0)
                    head_mx(1)
                    head_mx(2)
                if n + 9 < NT:
                    xtr(n + 9)
                    xev(n + 9)
            LEAD = 3
            for h in range(NH):
                parts = [(0, 2), (2, 2)] if h == NH - 1 else [(0, NJ)]
                for i, (t0, tn) in enumerate(parts):
                    head_prod(h, t0, tn)
                if h + LEAD < NH:
                    head_mx(h + LEAD)
                for i, (t0, tn) in enumerate(parts):
                    head_out(h, t0, tn, "v" if i == 1 else "s")
